import numpy as np
import ml_dtypes


def mxq(x, axis, fmt="e4m3"):
    dtype, down = {"e4m3": (ml_dtypes.float8_e4m3fn, 7), "e5m2": (ml_dtypes.float8_e5m2, 14)}[fmt]
    v = np.moveaxis(np.asarray(x, np.float32).astype(ml_dtypes.bfloat16).astype(np.float64), axis, -1)
    blocks = v.reshape(v.shape[:-1] + (-1, 32))
    amax = np.abs(blocks).max(-1, keepdims=True)
    byte = np.maximum(np.where(amax > 0, np.frexp(amax)[1] - 1 + 127, 0) - down, 1)
    scale = np.exp2(byte - 127.0)
    codes = (blocks / scale).astype(np.float32).astype(dtype).astype(np.float64)
    return np.moveaxis((codes * scale).reshape(v.shape), -1, axis)


WIDE = False


def mx_kscale(k):
    if not WIDE:
        return np.ones(k)
    levels = np.array([10, -10, 5, -5, 0])
    if k % 512:
        return np.exp2(np.random.permutation(np.resize(levels, k // 32))).repeat(32)
    a = np.empty((k // 512, 16))
    for p in range(k // 512):
        a[p, :8] = np.random.permutation(np.resize(levels, 8))
        for g in range(8):
            far = levels[np.abs(levels - a[p, g]) >= 10]
            a[p, g + 8] = far[np.random.randint(len(far))]
    return np.exp2(a.ravel()).repeat(32)


BF16 = ml_dtypes.bfloat16


def bf(x):
    return np.asarray(x, np.float32).astype(BF16)


def f64(x):
    return np.asarray(x).astype(np.float64)


B, L, E, H, DH, RK, RD, MAXLEN = 4, 512, 8192, 16, 128, 2048, 128, 4096


def apply_rope(x, cos, sin):
    cos = cos[None, :, None, :]
    sin = sin[None, :, None, :]
    x1, x2 = x[..., 0::2], x[..., 1::2]
    out_real = x1 * cos - x2 * sin
    out_imag = x1 * sin + x2 * cos
    return np.stack([out_real, out_imag], axis=-1).reshape(x.shape)


def setup_inputs():
    s, t = mx_kscale(E), mx_kscale(RK)
    tc = np.concatenate([t, np.ones(RD)])
    return {"x": bf(np.random.standard_normal((B, L, E)) * s),
            "cos": bf(np.random.uniform(size=(L, RD // 2))),
            "sin": bf(np.random.uniform(size=(L, RD // 2))),
            "wkv_down": bf(np.random.standard_normal((E, RK + RD)) / np.sqrt(E) / s[:, None] * tc),
            "w_up": bf(np.random.standard_normal((RK, H * (2 * DH + RD))) / np.sqrt(RK) / t[:, None])}


def reference(x, cos, sin, wkv_down, w_up):
    kv_lat = mxq(f64(x), 2, "e4m3") @ mxq(f64(wkv_down), 0, "e4m3")
    c_kv = kv_lat[..., :RK]
    k_rope = kv_lat[..., RK:]
    k_rope = apply_rope(k_rope[:, :, None, :], f64(cos), f64(sin))[:, :, 0, :]
    up = (mxq(c_kv, 2, "e4m3") @ mxq(f64(w_up), 0, "e4m3")).reshape(B, L, H, 2 * DH + RD)
    k_head = up[..., :DH]
    v_head = up[..., DH:2 * DH]
    v_rope = up[..., 2 * DH:]
    k_rope_b = np.broadcast_to(k_rope[:, :, None, :], (B, L, H, RD))
    k = np.concatenate([k_head, k_rope_b], axis=-1)
    v = np.concatenate([v_head, v_rope], axis=-1)
    return k, v

@@ -1,0 +1,449 @@
+from contextlib import ExitStack
+
+import concourse.mybir as mybir
+from concourse.masks import make_identity
+
+F32 = mybir.dt.float32
+BF16 = mybir.dt.bfloat16
+U32 = mybir.dt.uint32
+U8 = mybir.dt.uint8
+FP8X4 = mybir.dt.float8_e4m3fn_x4
+MULT = mybir.AluOpType.mult
+ADD = mybir.AluOpType.add
+SUB = mybir.AluOpType.subtract
+
+P = 128
+FLOPS = 2 * 2048 * 8192 * 2176 + 2 * 2048 * 2048 * 6144
+
+R4_BUFS = 8
+R2_BUFS = 6
+RING = 6
+UNITS = 64
+X_LEAD = 3
+SORT_LEAD = 2
+QUANT_LAG = 2
+
+
+def sorted_unit(u):
+    return u % 2 == 0
+
+
+def tile_multiheadlatentattention_pa_l_kernel(tc, x, cos, sin, wkv_down, w_up, out_0, out_1):
+    nc = tc.nc
+    with ExitStack() as ctx:
+        sb = ctx.enter_context(tc.tile_pool(name="sb", bufs=1))
+        ps = ctx.enter_context(tc.psum_pool(name="ps", bufs=1))
+
+        def r4(shape, dtype, name):
+            t = sb.tile(shape, dtype, name=name, tag="r4", bufs=R4_BUFS, align_bytes=64)
+            return t
+
+        def r2(shape, dtype, name):
+            t = sb.tile(shape, dtype, name=name, tag="r2", bufs=R2_BUFS, align_bytes=64)
+            return t
+
+        def big(shape, dtype, name):
+            t = sb.tile(shape, dtype, name=name, tag="xc", bufs=16, align_bytes=64)
+            return t
+
+        def plane(shape, name):
+            t = sb.tile(shape, U8, name=name, tag="xs", bufs=4, align_bytes=64)
+            return t
+
+        def ck_slot(shape, name):
+            t = sb.tile(shape, U32, name=name, tag="ck", bufs=4, align_bytes=64)
+            return t
+
+        def bank(i, shape):
+            t = ps.tile(shape, F32, name="bank%d" % i, tag="b%d" % i, bufs=1)
+            return t
+
+        xf = x.flatten_outer_dims()
+
+        ident = sb.tile([P, P], F32, name="ident", tag="ident", bufs=1, align_bytes=64)
+        make_identity(nc, ident[:])
+        cos_sb = sb.tile([P, 4, 64], BF16, name="cos_sb", tag="cos_sb", bufs=1, align_bytes=64)
+        sin_sb = sb.tile([P, 4, 64], BF16, name="sin_sb", tag="sin_sb", bufs=1, align_bytes=64)
+        nc.scalar.dma_start(out=cos_sb[:], in_=cos.rearrange("(a p) j -> p a j", p=P))
+        nc.scalar.dma_start(out=sin_sb[:], in_=sin.rearrange("(a p) j -> p a j", p=P))
+        ctx.enter_context(tc.manual_schedule())
+
+        xc = [big([P, 2048], U32, "xc%d" % g) for g in range(16)]
+        xs = [plane([P, 2048], "xs%d" % gq) for gq in range(4)]
+        cks = sb.tile([P, 2048], U8, name="cks", tag="cks", bufs=1, align_bytes=64)
+        wxr = ck_slot([P, 16, 128], "wxr")
+        wrs = sb.tile([P, 4, 128], U8, name="wrs", tag="wrs", bufs=1, align_bytes=64)
+
+        xr, xsd, xt, gw = {}, {}, {}, {}
+
+        def load_x(u):
+            tt, q = divmod(u, 4)
+            t = r4([P, 2048], BF16, "xr")
+            nc.sync.dma_start(out=t[:], in_=xf[128 * tt : 128 * tt + 128, 2048 * q : 2048 * q + 2048])
+            xr[u] = t
+
+        def sort_x(u):
+            if sorted_unit(u):
+                t = r4([P, 4, 2, 128], F32, "xsd")
+                nc.vector.tensor_copy(
+                    out=t[:], in_=xr.pop(u)[:].bitcast(F32).rearrange("a (g p u) -> a g u p", g=4, u=2)
+                )
+                xsd[u] = t
+
+        def transpose_x(u):
+            if sorted_unit(u):
+                src = xsd.pop(u)
+            else:
+                src = xr.pop(u)[:].bitcast(F32)
+            for half in range(2):
+                b = bank((2 * u + half) % 6, [P, 2, 2, 128])
+                for g2 in range(2):
+                    gl = 2 * half + g2
+                    for uu in range(2):
+                        if sorted_unit(u):
+                            words = src[:, gl, uu, :]
+                        else:
+                            words = src[:, 256 * gl + uu : 256 * (gl + 1) : 2]
+                        nc.tensor.transpose(b[:, g2, uu, :], words, ident[:])
+                xt[(u, half)] = b
+
+        def copy_x(u):
+            for half in range(2):
+                t = r2([P, 2, 128, 2], F32, "gw")
+                nc.scalar.copy(out=t[:], in_=xt.pop((u, half))[:].rearrange("p g u c -> p g c u"))
+                gw[(u, half)] = t
+
+        def quant_x(u):
+            tt, q = divmod(u, 4)
+            for half in range(2):
+                t = gw.pop((u, half))
+                for g2 in range(2):
+                    g = 4 * q + 2 * half + g2
+                    k = 4 * (g % 4)
+                    nc.vector.quantize_mx(
+                        out=xc[g][:, 128 * tt : 128 * tt + 128].bitcast(FP8X4),
+                        scales=xs[g // 4][k:P, 128 * tt : 128 * tt + 128],
+                        in_=t[:, g2].rearrange("p c u -> p (c u)").bitcast(BF16),
+                    )
+
+        rr, rg = {}, {}
+
+        def rope_w_load(g4):
+            t = r4([P, 4, 4, 128], BF16, "rr")
+            for gl in range(4):
+                g = 4 * g4 + gl
+                nc.sync.dma_start(
+                    out=t[:, gl], in_=wkv_down[512 * g : 512 * g + 512, 2048:2176].rearrange("(p j) c -> p j c", j=4)
+                )
+            rr[g4] = t
+
+        def rope_w_inter(g4):
+            t = r4([P, 4, 128, 4], BF16, "rg")
+            nc.vector.tensor_copy(out=t[:], in_=rr.pop(g4)[:].rearrange("p g j c -> p g c j"))
+            rg[g4] = t
+
+        def rope_w_quant(g4):
+            t = rg.pop(g4)
+            for gl in range(4):
+                nc.vector.quantize_mx(
+                    out=wxr[:, 4 * g4 + gl, :].bitcast(FP8X4),
+                    scales=wrs[4 * gl : P, g4, :],
+                    in_=t[:, gl].rearrange("p c j -> p (c j)"),
+                )
+
+        rp, krs = {}, {}
+
+        def rope_mm(tt):
+            n, a = divmod(tt, 4)
+            if a == 0:
+                rp[n] = bank(6 + n % 2, [P, 4, 128])
+            cols = slice(128 * tt, 128 * tt + 128)
+            for g in range(16):
+                k = 4 * (g % 4)
+                nc.tensor.matmul_mx(
+                    out=rp[n][:, a, :],
+                    lhsT=xc[g][:, cols].bitcast(FP8X4),
+                    lhsT_scale=xs[g // 4][k:P, cols],
+                    rhs=wxr[:, g, :].bitcast(FP8X4),
+                    rhs_scale=wrs[k:P, g // 4, :],
+                    start=(g == 0),
+                    stop=(g == 15),
+                )
+
+        def rope_math(n):
+            r = rp.pop(n)[:].rearrange("p a (j e) -> p a j e", e=2)
+            kr = sb.tile([P, 4, 64, 2], F32, name="kr", tag="kr", bufs=4, align_bytes=64)
+            tmp = [sb.tile([P, 4, 64], F32, name="tmp%d" % i, tag="tmp%d" % i, bufs=1, align_bytes=64) for i in range(4)]
+            nc.vector.tensor_tensor(out=tmp[0][:], in0=r[:, :, :, 0], in1=cos_sb[:], op=MULT)
+            nc.vector.tensor_tensor(out=tmp[1][:], in0=r[:, :, :, 1], in1=sin_sb[:], op=MULT)
+            nc.vector.tensor_tensor(out=tmp[2][:], in0=r[:, :, :, 0], in1=sin_sb[:], op=MULT)
+            nc.vector.tensor_tensor(out=tmp[3][:], in0=r[:, :, :, 1], in1=cos_sb[:], op=MULT)
+            nc.vector.tensor_tensor(out=kr[:, :, :, 0], in0=tmp[0][:], in1=tmp[1][:], op=SUB)
+            nc.vector.tensor_tensor(out=kr[:, :, :, 1], in0=tmp[2][:], in1=tmp[3][:], op=ADD)
+            krs[n] = kr
+
+        def rope_store(tt):
+            n, a = divmod(tt, 4)
+            nc.gpsimd.dma_start(
+                out=out_0[n, 128 * a : 128 * a + 128, :, 128:256],
+                in_=krs[n][:, a].rearrange("p j e -> p (j e)").unsqueeze(1).to_broadcast([P, 16, 128]),
+            )
+
+        wr, wg, ring = {}, {}, {}
+
+        def w_load(i):
+            s, g = divmod(i, 16)
+            t = r4([P, 4, 512], BF16, "wr")
+            gg = s // 2
+            nc.sync.dma_start(
+                out=t[:],
+                in_=wkv_down[512 * g : 512 * g + 512, 512 * gg : 512 * gg + 512].rearrange("(p j) c -> p j c", j=4),
+            )
+            wr[i] = t
+
+        def w_inter(i):
+            h = (i // 16) % 2
+            t = r2([P, 1024], BF16, "wg")
+            nc.scalar.copy(
+                out=t[:].rearrange("p (t m j) -> p t m j", t=2, j=4),
+                in_=wr.pop(i)[:].rearrange("p j (m t) -> p t m j", t=4)[:, 2 * h : 2 * h + 2],
+            )
+            wg[i] = t
+
+        def w_quant(i):
+            rc = sb.tile([P, 256], U32, name="rc", tag="rc", bufs=RING, align_bytes=64)
+            rs = sb.tile([P, 256], U8, name="rs", tag="rs", bufs=RING, align_bytes=64)
+            nc.vector.quantize_mx(out=rc[:].bitcast(FP8X4), scales=rs[:], in_=wg.pop(i)[:])
+            ring[i] = (rc, rs)
+
+        acc = {}
+        BANK_ORDER = {
+            False: [(tl, n) for tl in range(2) for n in range(4)],
+            True: [(tl, n) for n in range(4) for tl in range(2)],
+        }
+
+        def sweep_mm(i):
+            s, g = divmod(i, 16)
+            rc, rs = ring.pop(i)
+            k = 4 * (g % 4)
+            for tl, n in BANK_ORDER[s == 7]:
+                if True:
+                    if g == 0:
+                        acc[(tl, n)] = bank(BANK_ORDER[s == 7].index((tl, n)), [P, 512])
+                    nc.tensor.matmul_mx(
+                        out=acc[(tl, n)][:],
+                        lhsT=rc[:, 128 * tl : 128 * tl + 128].bitcast(FP8X4),
+                        lhsT_scale=rs[:, 128 * tl : 128 * tl + 128],
+                        rhs=xc[g][:, 512 * n : 512 * n + 512].bitcast(FP8X4),
+                        rhs_scale=xs[g // 4][k:P, 512 * n : 512 * n + 512],
+                        start=(g == 0),
+                        stop=(g == 15),
+                    )
+
+        st, ck = {}, {}
+
+        def evac(s):
+            h = s % 2
+            for tl, n in BANK_ORDER[s == 7]:
+                if h == 0 and tl == 0:
+                    st[n] = r4([P, 4, 512], BF16, "st")
+                dst = st[n][:, 2 * h + tl, :]
+                if n % 2 == 0 or s == 7:
+                    nc.scalar.copy(out=dst, in_=acc.pop((tl, n))[:])
+                else:
+                    nc.vector.tensor_copy(out=dst, in_=acc.pop((tl, n))[:])
+
+        cg = {}
+
+        def ck_inter(gg, piece):
+            n, i2 = divmod(piece, 2)
+            t = r2([P, 256, 4], BF16, "cg")
+            nc.vector.tensor_copy(out=t[:], in_=st[n][:, :, 256 * i2 : 256 * i2 + 256].rearrange("p t c -> p c t"))
+            cg[piece] = t
+
+        def ck_quant(gg, piece):
+            if piece == 0:
+                ck[gg] = ck_slot([P, 2048], "ck%d" % gg)
+            cols = slice(256 * piece, 256 * piece + 256)
+            nc.vector.quantize_mx(
+                out=ck[gg][:, cols].bitcast(FP8X4),
+                scales=cks[4 * gg : P, cols],
+                in_=cg.pop(piece)[:].rearrange("p c t -> p (c t)"),
+            )
+
+        UNIT_MOVES = (
+            ((0, 2, 0, 3), (2, 2, 1, 1)),
+            ((0, 1, 2, 1), (1, 2, 0, 1), (3, 1, 3, 1)),
+            ((0, 1, 1, 1), (1, 1, 0, 1), (2, 2, 2, 1)),
+        )
+        ur, ug, wu, wus = {}, {}, {}, {}
+
+        def u_load(j):
+            cb, gg = divmod(j, 4)
+            t = big([P, 4, 512], BF16, "ur")
+            nc.sync.dma_start(
+                out=t[:],
+                in_=w_up[512 * gg : 512 * gg + 512, 512 * cb : 512 * cb + 512].rearrange("(p j) c -> p j c", j=4),
+            )
+            ur[j] = t
+
+        def u_inter(j):
+            cb = j // 4
+            src = ur.pop(j)[:].rearrange("p j (s c) -> p s c j", s=4)
+            t = big([P, 4, 128, 4], BF16, "ug")
+            for d0, cnt, s0, step in UNIT_MOVES[cb % 3]:
+                if j < 12 and j % 3 == 2:
+                    nc.scalar.copy(out=t[:, d0 : d0 + cnt], in_=src[:, s0 : s0 + (cnt - 1) * step + 1 : step])
+                else:
+                    nc.vector.tensor_copy(out=t[:, d0 : d0 + cnt], in_=src[:, s0 : s0 + (cnt - 1) * step + 1 : step])
+            ug[j] = t
+
+        def u_quant(j):
+            cb, gg = divmod(j, 4)
+            if gg == 0:
+                wu[cb] = big([P, 4, 512], U32, "wu%d" % cb)
+                if cb % 3 == 0:
+                    wus[cb // 3] = plane([P, 1536], "wus%d" % (cb // 3))
+            nc.vector.quantize_mx(
+                out=wu[cb][:, gg, :].bitcast(FP8X4),
+                scales=wus[cb // 3][4 * gg : P, 512 * (cb % 3) : 512 * (cb % 3) + 512],
+                in_=ug.pop(j)[:].rearrange("p s c j -> p (s c j)"),
+            )
+
+        def pu(t, inter=True):
+            if inter and 0 <= t - 2 < 48:
+                u_inter(t - 2)
+            if 0 <= t - 3 < 48:
+                u_quant(t - 3)
+            if t < 48:
+                u_load(t)
+
+        cell = {}
+
+        def up_mm(ci, gg):
+            c, cbl = divmod(ci, 3)
+            hg, tt = divmod(c, 16)
+            if gg == 0:
+                cell[ci] = bank(ci % 8, [P, 512])
+            cols = slice(128 * tt, 128 * tt + 128)
+            nc.tensor.matmul_mx(
+                out=cell[ci][:],
+                lhsT=ck[gg][:, cols].bitcast(FP8X4),
+                lhsT_scale=cks[4 * gg : P, cols],
+                rhs=wu[3 * hg + cbl][:, gg, :].bitcast(FP8X4),
+                rhs_scale=wus[hg][4 * gg : P, 512 * cbl : 512 * cbl + 512],
+                start=(gg == 0),
+                stop=(gg == 3),
+            )
+
+        K_COLS = (256, 128, 128)
+
+        def up_out(c):
+            hg, tt = divmod(c, 16)
+            b, a = divmod(tt, 4)
+            ko = r2([P, 512], F32, "ko")
+            vo = r4([P, 1024], F32, "vo")
+            k0, v0 = 0, 0
+            for cbl in range(3):
+                src = cell.pop(3 * c + cbl)
+                kc = K_COLS[cbl]
+                nc.scalar.copy(out=ko[:, k0 : k0 + kc], in_=src[:, 0:kc])
+                nc.scalar.copy(out=vo[:, v0 : v0 + 512 - kc], in_=src[:, kc:512])
+                k0 += kc
+                v0 += 512 - kc
+            rows = slice(128 * a, 128 * a + 128)
+            nc.sync.dma_start(
+                out=out_0[b, rows, 4 * hg : 4 * hg + 4, 0:128], in_=ko[:].rearrange("p (h c) -> p h c", h=4)
+            )
+            nc.sync.dma_start(out=out_1[b, rows, 4 * hg : 4 * hg + 4, :].rearrange("l h c -> l (h c)"), in_=vo[:])
+
+        ROPE_LOAD_AFTER = {2: 0, 5: 1, 8: 2, 11: 3}
+        ROPE_MM_AFTER = {19: (0, 1), 21: (2, 3), 26: (4, 5)}
+        for tt in range(7, 16, 2):
+            ROPE_MM_AFTER[4 * tt + 6] = (tt - 1, tt)
+        ROPE_MATH_AFTER = {24: 0, 37: 1, 53: 2, 69: 3}
+
+        for u in range(X_LEAD):
+            load_x(u)
+        for u in range(SORT_LEAD):
+            sort_x(u)
+        for s in range(UNITS + 7):
+            if s + X_LEAD < UNITS:
+                load_x(s + X_LEAD)
+            if s in ROPE_LOAD_AFTER:
+                rope_w_load(ROPE_LOAD_AFTER[s])
+            if s - 3 in ROPE_LOAD_AFTER:
+                rope_w_inter(ROPE_LOAD_AFTER[s - 3])
+            if s + SORT_LEAD < UNITS:
+                sort_x(s + SORT_LEAD)
+            if s < UNITS:
+                transpose_x(s)
+            if 0 <= s - 1 < UNITS:
+                copy_x(s - 1)
+            if 0 <= s - QUANT_LAG < UNITS:
+                quant_x(s - QUANT_LAG)
+            if s - 5 in ROPE_LOAD_AFTER:
+                rope_w_quant(ROPE_LOAD_AFTER[s - 5])
+            if s in ROPE_MM_AFTER:
+                for tt in ROPE_MM_AFTER[s]:
+                    rope_mm(tt)
+            if s in ROPE_MATH_AFTER:
+                rope_math(ROPE_MATH_AFTER[s])
+            if s >= UNITS - 3 and s - (UNITS - 3) < 6:
+                w_load(s - (UNITS - 3))
+            if s >= UNITS and s - UNITS < 3:
+                w_inter(s - UNITS)
+            if s >= UNITS + 1 and s - UNITS - 1 < 2:
+                w_quant(s - UNITS - 1)
+
+        pieces = []
+        for i in range(128):
+            s, g = divmod(i, 16)
+            if i + 6 < 128:
+                w_load(i + 6)
+            if i + 3 < 128:
+                w_inter(i + 3)
+            if pieces:
+                ck_inter(pieces[0][0], pieces[0][1])
+            if i + 2 < 128:
+                w_quant(i + 2)
+            if pieces:
+                gg, piece = pieces.pop(0)
+                ck_quant(gg, piece)
+            sweep_mm(i)
+            if i % 4 == 2 and i // 4 < 16:
+                rope_store(i // 4)
+            if i >= 113:
+                pu(i - 113, i < 127)
+            if g == 15:
+                evac(s)
+                if s % 2 == 1:
+                    pieces.extend([(s // 2, piece) for piece in range(8)])
+
+        for gg, piece in pieces:
+            ck_inter(gg, piece)
+            if piece > 0:
+                ck_quant(gg, piece - 1)
+            if piece == 2:
+                u_inter(12)
+        ck_quant(3, 7)
+
+        for gg in range(3):
+            for ci in range(8):
+                up_mm(ci, gg)
+        for ci in range(8):
+            up_mm(ci, 3)
+        up_out(0)
+        up_out(1)
+        pu(15)
+        pu(16)
+        for gg in range(4):
+            up_mm(8, gg)
+        up_out(2)
+        pu(17)
+        for c in range(3, 64):
+            for cbl in range(3):
+                for gg in range(4):
+                    up_mm(3 * c + cbl, gg)
+            up_out(c)
+            pu(15 + c)

@@ -19,7 +19,7 @@ R4_BUFS = 8
 R2_BUFS = 6
 RING = 6
 UNITS = 64
-X_LEAD = 3
+X_LEAD = 5
 SORT_LEAD = 2
 QUANT_LAG = 2
 
@@ -50,8 +50,8 @@ def tile_multiheadlatentattention_pa_l_kernel(tc, x, cos, sin, wkv_down, w_up, o
             t = sb.tile(shape, U8, name=name, tag="xs", bufs=4, align_bytes=64)
             return t
 
-        def ck_slot(shape, name):
-            t = sb.tile(shape, U32, name=name, tag="ck", bufs=4, align_bytes=64)
+        def ck_slot(shape, name, dtype=U32):
+            t = sb.tile(shape, dtype, name=name, tag="ck", bufs=4, align_bytes=64)
             return t
 
         def bank(i, shape):
@@ -129,7 +129,7 @@ def tile_multiheadlatentattention_pa_l_kernel(tc, x, cos, sin, wkv_down, w_up, o
         rr, rg = {}, {}
 
         def rope_w_load(g4):
-            t = r4([P, 4, 4, 128], BF16, "rr")
+            t = ck_slot([P, 4, 4, 128], "rr", BF16)
             for gl in range(4):
                 g = 4 * g4 + gl
                 nc.sync.dma_start(
@@ -138,7 +138,7 @@ def tile_multiheadlatentattention_pa_l_kernel(tc, x, cos, sin, wkv_down, w_up, o
             rr[g4] = t
 
         def rope_w_inter(g4):
-            t = r4([P, 4, 128, 4], BF16, "rg")
+            t = ck_slot([P, 4, 128, 4], "rg", BF16)
             nc.vector.tensor_copy(out=t[:], in_=rr.pop(g4)[:].rearrange("p g j c -> p g c j"))
             rg[g4] = t
 
@@ -184,7 +184,7 @@ def tile_multiheadlatentattention_pa_l_kernel(tc, x, cos, sin, wkv_down, w_up, o
 
         def rope_store(tt):
             n, a = divmod(tt, 4)
-            nc.gpsimd.dma_start(
+            nc.sync.dma_start(
                 out=out_0[n, 128 * a : 128 * a + 128, :, 128:256],
                 in_=krs[n][:, a].rearrange("p j e -> p (j e)").unsqueeze(1).to_broadcast([P, 16, 128]),
             )
@@ -204,10 +204,12 @@ def tile_multiheadlatentattention_pa_l_kernel(tc, x, cos, sin, wkv_down, w_up, o
         def w_inter(i):
             h = (i // 16) % 2
             t = r2([P, 1024], BF16, "wg")
-            nc.scalar.copy(
-                out=t[:].rearrange("p (t m j) -> p t m j", t=2, j=4),
-                in_=wr.pop(i)[:].rearrange("p j (m t) -> p t m j", t=4)[:, 2 * h : 2 * h + 2],
-            )
+            dst = t[:].rearrange("p (t m j) -> p t m j", t=2, j=4)
+            src = wr.pop(i)[:].rearrange("p j (m t) -> p t m j", t=4)[:, 2 * h : 2 * h + 2]
+            if i % 2 == 0 or i >= 112:
+                nc.scalar.copy(out=dst, in_=src)
+            else:
+                nc.vector.tensor_copy(out=dst, in_=src)
             wg[i] = t
 
         def w_quant(i):
@@ -347,8 +349,12 @@ def tile_multiheadlatentattention_pa_l_kernel(tc, x, cos, sin, wkv_down, w_up, o
             for cbl in range(3):
                 src = cell.pop(3 * c + cbl)
                 kc = K_COLS[cbl]
-                nc.scalar.copy(out=ko[:, k0 : k0 + kc], in_=src[:, 0:kc])
-                nc.scalar.copy(out=vo[:, v0 : v0 + 512 - kc], in_=src[:, kc:512])
+                if cbl == 1:
+                    nc.vector.tensor_copy(out=ko[:, k0 : k0 + kc], in_=src[:, 0:kc])
+                    nc.vector.tensor_copy(out=vo[:, v0 : v0 + 512 - kc], in_=src[:, kc:512])
+                else:
+                    nc.scalar.copy(out=ko[:, k0 : k0 + kc], in_=src[:, 0:kc])
+                    nc.scalar.copy(out=vo[:, v0 : v0 + 512 - kc], in_=src[:, kc:512])
                 k0 += kc
                 v0 += 512 - kc
             rows = slice(128 * a, 128 * a + 128)
@@ -411,8 +417,8 @@ def tile_multiheadlatentattention_pa_l_kernel(tc, x, cos, sin, wkv_down, w_up, o
                 gg, piece = pieces.pop(0)
                 ck_quant(gg, piece)
             sweep_mm(i)
-            if i % 4 == 2 and i // 4 < 16:
-                rope_store(i // 4)
+            if i % 7 == 3 and i // 7 < 16:
+                rope_store(i // 7)
             if i >= 113:
                 pu(i - 113, i < 127)
             if g == 15:

@@ -15,17 +15,18 @@ SUB = mybir.AluOpType.subtract
 P = 128
 FLOPS = 2 * 2048 * 8192 * 2176 + 2 * 2048 * 2048 * 6144
 
-R4_BUFS = 8
+R4_BUFS = 9
 R2_BUFS = 6
 RING = 6
 UNITS = 64
-X_LEAD = 5
+X_LEAD = 3
 SORT_LEAD = 2
 QUANT_LAG = 2
+W_LAG = 2
 
 
 def sorted_unit(u):
-    return u % 2 == 0
+    return u >= 32
 
 
 def tile_multiheadlatentattention_pa_l_kernel(tc, x, cos, sin, wkv_down, w_up, out_0, out_1):
@@ -51,7 +52,7 @@ def tile_multiheadlatentattention_pa_l_kernel(tc, x, cos, sin, wkv_down, w_up, o
             return t
 
         def ck_slot(shape, name, dtype=U32):
-            t = sb.tile(shape, dtype, name=name, tag="ck", bufs=4, align_bytes=64)
+            t = sb.tile(shape, dtype, name=name, tag="ck", bufs=5, align_bytes=64)
             return t
 
         def bank(i, shape):
@@ -71,7 +72,8 @@ def tile_multiheadlatentattention_pa_l_kernel(tc, x, cos, sin, wkv_down, w_up, o
         xc = [big([P, 2048], U32, "xc%d" % g) for g in range(16)]
         xs = [plane([P, 2048], "xs%d" % gq) for gq in range(4)]
         cks = sb.tile([P, 2048], U8, name="cks", tag="cks", bufs=1, align_bytes=64)
-        wxr = ck_slot([P, 16, 128], "wxr")
+        wxr = {}
+        wxs = sb.tile([P, 4, 512], U8, name="wxs", tag="wxs", bufs=1, align_bytes=64)
         wrs = sb.tile([P, 4, 128], U8, name="wrs", tag="wrs", bufs=1, align_bytes=64)
 
         xr, xsd, xt, gw = {}, {}, {}, {}
@@ -96,7 +98,7 @@ def tile_multiheadlatentattention_pa_l_kernel(tc, x, cos, sin, wkv_down, w_up, o
             else:
                 src = xr.pop(u)[:].bitcast(F32)
             for half in range(2):
-                b = bank((2 * u + half) % 6, [P, 2, 2, 128])
+                b = bank((2 * u + half) % 4, [P, 2, 2, 128])
                 for g2 in range(2):
                     gl = 2 * half + g2
                     for uu in range(2):
@@ -129,7 +131,7 @@ def tile_multiheadlatentattention_pa_l_kernel(tc, x, cos, sin, wkv_down, w_up, o
         rr, rg = {}, {}
 
         def rope_w_load(g4):
-            t = ck_slot([P, 4, 4, 128], "rr", BF16)
+            t = r4([P, 4, 4, 128], BF16, "rr")
             for gl in range(4):
                 g = 4 * g4 + gl
                 nc.sync.dma_start(
@@ -138,15 +140,17 @@ def tile_multiheadlatentattention_pa_l_kernel(tc, x, cos, sin, wkv_down, w_up, o
             rr[g4] = t
 
         def rope_w_inter(g4):
-            t = ck_slot([P, 4, 128, 4], "rg", BF16)
+            t = r4([P, 4, 128, 4], BF16, "rg")
             nc.vector.tensor_copy(out=t[:], in_=rr.pop(g4)[:].rearrange("p g j c -> p g c j"))
             rg[g4] = t
 
         def rope_w_quant(g4):
             t = rg.pop(g4)
+            if g4 % 2 == 0:
+                wxr[g4 // 2] = r4([P, 8, 128], U32, "wxr")
             for gl in range(4):
                 nc.vector.quantize_mx(
-                    out=wxr[:, 4 * g4 + gl, :].bitcast(FP8X4),
+                    out=wxr[g4 // 2][:, 4 * (g4 % 2) + gl, :].bitcast(FP8X4),
                     scales=wrs[4 * gl : P, g4, :],
                     in_=t[:, gl].rearrange("p c j -> p (c j)"),
                 )
@@ -156,7 +160,7 @@ def tile_multiheadlatentattention_pa_l_kernel(tc, x, cos, sin, wkv_down, w_up, o
         def rope_mm(tt):
             n, a = divmod(tt, 4)
             if a == 0:
-                rp[n] = bank(6 + n % 2, [P, 4, 128])
+                rp[n] = bank(n, [P, 4, 128])
             cols = slice(128 * tt, 128 * tt + 128)
             for g in range(16):
                 k = 4 * (g % 4)
@@ -164,7 +168,7 @@ def tile_multiheadlatentattention_pa_l_kernel(tc, x, cos, sin, wkv_down, w_up, o
                     out=rp[n][:, a, :],
                     lhsT=xc[g][:, cols].bitcast(FP8X4),
                     lhsT_scale=xs[g // 4][k:P, cols],
-                    rhs=wxr[:, g, :].bitcast(FP8X4),
+                    rhs=wxr[g // 8][:, g % 8, :].bitcast(FP8X4),
                     rhs_scale=wrs[k:P, g // 4, :],
                     start=(g == 0),
                     stop=(g == 15),
@@ -172,24 +176,26 @@ def tile_multiheadlatentattention_pa_l_kernel(tc, x, cos, sin, wkv_down, w_up, o
 
         def rope_math(n):
             r = rp.pop(n)[:].rearrange("p a (j e) -> p a j e", e=2)
-            kr = sb.tile([P, 4, 64, 2], F32, name="kr", tag="kr", bufs=4, align_bytes=64)
-            tmp = [sb.tile([P, 4, 64], F32, name="tmp%d" % i, tag="tmp%d" % i, bufs=1, align_bytes=64) for i in range(4)]
+            if n == 0:
+                krs[0] = ck_slot([P, 16, 64, 2], "krall", F32)
+            kr = krs[0][:, 4 * n : 4 * n + 4]
+            tmp = [sb.tile([P, 4, 64], F32, name="tmp%d" % i, tag="rc", bufs=RING, align_bytes=64) for i in range(4)]
             nc.vector.tensor_tensor(out=tmp[0][:], in0=r[:, :, :, 0], in1=cos_sb[:], op=MULT)
             nc.vector.tensor_tensor(out=tmp[1][:], in0=r[:, :, :, 1], in1=sin_sb[:], op=MULT)
             nc.vector.tensor_tensor(out=tmp[2][:], in0=r[:, :, :, 0], in1=sin_sb[:], op=MULT)
             nc.vector.tensor_tensor(out=tmp[3][:], in0=r[:, :, :, 1], in1=cos_sb[:], op=MULT)
             nc.vector.tensor_tensor(out=kr[:, :, :, 0], in0=tmp[0][:], in1=tmp[1][:], op=SUB)
             nc.vector.tensor_tensor(out=kr[:, :, :, 1], in0=tmp[2][:], in1=tmp[3][:], op=ADD)
-            krs[n] = kr
 
         def rope_store(tt):
             n, a = divmod(tt, 4)
             nc.sync.dma_start(
                 out=out_0[n, 128 * a : 128 * a + 128, :, 128:256],
-                in_=krs[n][:, a].rearrange("p j e -> p (j e)").unsqueeze(1).to_broadcast([P, 16, 128]),
+                in_=krs[0][:, tt].rearrange("p j e -> p (j e)").unsqueeze(1).to_broadcast([P, 16, 128]),
             )
 
         wr, wg, ring = {}, {}, {}
+        st, ck = {}, {}
 
         def w_load(i):
             s, g = divmod(i, 16)
@@ -218,6 +224,52 @@ def tile_multiheadlatentattention_pa_l_kernel(tc, x, cos, sin, wkv_down, w_up, o
             nc.vector.quantize_mx(out=rc[:].bitcast(FP8X4), scales=rs[:], in_=wg.pop(i)[:])
             ring[i] = (rc, rs)
 
+        wxh = {}
+
+        def main_w_inter(g, h):
+            t = r2([P, 1024], BF16, "wg")
+            dst = t[:].rearrange("p (t m j) -> p t m j", t=2, j=4)
+            src = wr[g][:].rearrange("p j (m t) -> p t m j", t=4)[:, 2 * h : 2 * h + 2]
+            if h == 0:
+                nc.scalar.copy(out=dst, in_=src)
+            else:
+                nc.vector.tensor_copy(out=dst, in_=src)
+                wr.pop(g)
+            wg[(g, h)] = t
+
+        def main_w_quant(g, h):
+            if g % 8 == 0:
+                wxh[(h, g // 8)] = ck_slot([P, 8, 256], "wxh")
+            nc.vector.quantize_mx(
+                out=wxh[(h, g // 8)][:, g % 8, :].bitcast(FP8X4),
+                scales=wxs[4 * (g % 4) : P, g // 4, 256 * h : 256 * h + 256],
+                in_=wg.pop((g, h))[:],
+            )
+
+        def main_mm(n, g):
+            k = 4 * (g % 4)
+            for t in range(4):
+                h, tl = divmod(t, 2)
+                if g == 0:
+                    acc[(t, n)] = bank(4 + t, [P, 512])
+                nc.tensor.matmul_mx(
+                    out=acc[(t, n)][:],
+                    lhsT=wxh[(h, g // 8)][:, g % 8, 128 * tl : 128 * tl + 128].bitcast(FP8X4),
+                    lhsT_scale=wxs[k:P, g // 4, 256 * h + 128 * tl : 256 * h + 128 * tl + 128],
+                    rhs=xc[g][:, 512 * n : 512 * n + 512].bitcast(FP8X4),
+                    rhs_scale=xs[g // 4][k:P, 512 * n : 512 * n + 512],
+                    start=(g == 0),
+                    stop=(g == 15),
+                )
+
+        def main_evac(n):
+            st[n] = r4([P, 4, 512], BF16, "st")
+            for t in range(4):
+                if t % 2 == 0:
+                    nc.scalar.copy(out=st[n][:, t, :], in_=acc.pop((t, n))[:])
+                else:
+                    nc.vector.tensor_copy(out=st[n][:, t, :], in_=acc.pop((t, n))[:])
+
         acc = {}
         BANK_ORDER = {
             False: [(tl, n) for tl in range(2) for n in range(4)],
@@ -231,7 +283,7 @@ def tile_multiheadlatentattention_pa_l_kernel(tc, x, cos, sin, wkv_down, w_up, o
             for tl, n in BANK_ORDER[s == 7]:
                 if True:
                     if g == 0:
-                        acc[(tl, n)] = bank(BANK_ORDER[s == 7].index((tl, n)), [P, 512])
+                        acc[(tl, n)] = bank((4 + BANK_ORDER[s == 7].index((tl, n))) % 8, [P, 512])
                     nc.tensor.matmul_mx(
                         out=acc[(tl, n)][:],
                         lhsT=rc[:, 128 * tl : 128 * tl + 128].bitcast(FP8X4),
@@ -241,8 +293,6 @@ def tile_multiheadlatentattention_pa_l_kernel(tc, x, cos, sin, wkv_down, w_up, o
                         start=(g == 0),
                         stop=(g == 15),
                     )
-
-        st, ck = {}, {}
 
         def evac(s):
             h = s % 2
@@ -326,7 +376,7 @@ def tile_multiheadlatentattention_pa_l_kernel(tc, x, cos, sin, wkv_down, w_up, o
             c, cbl = divmod(ci, 3)
             hg, tt = divmod(c, 16)
             if gg == 0:
-                cell[ci] = bank(ci % 8, [P, 512])
+                cell[ci] = bank((ci + 4) % 8, [P, 512])
             cols = slice(128 * tt, 128 * tt + 128)
             nc.tensor.matmul_mx(
                 out=cell[ci][:],
@@ -363,47 +413,76 @@ def tile_multiheadlatentattention_pa_l_kernel(tc, x, cos, sin, wkv_down, w_up, o
             )
             nc.sync.dma_start(out=out_1[b, rows, 4 * hg : 4 * hg + 4, :].rearrange("l h c -> l (h c)"), in_=vo[:])
 
-        ROPE_LOAD_AFTER = {2: 0, 5: 1, 8: 2, 11: 3}
-        ROPE_MM_AFTER = {19: (0, 1), 21: (2, 3), 26: (4, 5)}
-        for tt in range(7, 16, 2):
-            ROPE_MM_AFTER[4 * tt + 6] = (tt - 1, tt)
-        ROPE_MATH_AFTER = {24: 0, 37: 1, 53: 2, 69: 3}
-
-        for u in range(X_LEAD):
-            load_x(u)
-        for u in range(SORT_LEAD):
-            sort_x(u)
-        for s in range(UNITS + 7):
-            if s + X_LEAD < UNITS:
-                load_x(s + X_LEAD)
-            if s in ROPE_LOAD_AFTER:
-                rope_w_load(ROPE_LOAD_AFTER[s])
-            if s - 3 in ROPE_LOAD_AFTER:
-                rope_w_inter(ROPE_LOAD_AFTER[s - 3])
-            if s + SORT_LEAD < UNITS:
-                sort_x(s + SORT_LEAD)
-            if s < UNITS:
-                transpose_x(s)
-            if 0 <= s - 1 < UNITS:
-                copy_x(s - 1)
-            if 0 <= s - QUANT_LAG < UNITS:
-                quant_x(s - QUANT_LAG)
-            if s - 5 in ROPE_LOAD_AFTER:
-                rope_w_quant(ROPE_LOAD_AFTER[s - 5])
-            if s in ROPE_MM_AFTER:
-                for tt in ROPE_MM_AFTER[s]:
-                    rope_mm(tt)
-            if s in ROPE_MATH_AFTER:
-                rope_math(ROPE_MATH_AFTER[s])
-            if s >= UNITS - 3 and s - (UNITS - 3) < 6:
-                w_load(s - (UNITS - 3))
-            if s >= UNITS and s - UNITS < 3:
-                w_inter(s - UNITS)
-            if s >= UNITS + 1 and s - UNITS - 1 < 2:
-                w_quant(s - UNITS - 1)
-
+        W_ROUND = [(3 * g) // 4 for g in range(16)]
+        ROPE_W_ROUND = {30: 0, 31: 1, 32: 2, 33: 3}
         pieces = []
-        for i in range(128):
+
+        for u in range(X_LEAD + 2):
+            load_x(u)
+        sort_x(0)
+        sort_x(1)
+        for r in range(40):
+            for u in (2 * r - 2, 2 * r - 1):
+                if 0 <= u < UNITS:
+                    quant_x(u)
+            if r < 32:
+                transpose_x(2 * r)
+                transpose_x(2 * r + 1)
+                copy_x(2 * r)
+                copy_x(2 * r + 1)
+            for u in (2 * r + X_LEAD + 2, 2 * r + X_LEAD + 3):
+                if u < UNITS:
+                    load_x(u)
+            for g in range(16):
+                if W_ROUND[g] == r:
+                    w_load(g)
+            if r in ROPE_W_ROUND:
+                rope_w_load(ROPE_W_ROUND[r])
+            if r >= 38:
+                w_load(32 + 2 * (r - 38))
+                w_load(33 + 2 * (r - 38))
+            for g in range(16):
+                if W_ROUND[g] + W_LAG == r:
+                    main_w_inter(g, 0)
+                    main_w_inter(g, 1)
+                    main_w_quant(g, 0)
+                    main_w_quant(g, 1)
+            if r - 2 in ROPE_W_ROUND:
+                rope_w_inter(ROPE_W_ROUND[r - 2])
+            if pieces:
+                ck_inter(pieces[0][0], pieces[0][1])
+            for u in (2 * r + 2, 2 * r + 3):
+                if u < UNITS:
+                    sort_x(u)
+            if r - 3 in ROPE_W_ROUND:
+                rope_w_quant(ROPE_W_ROUND[r - 3])
+            if pieces:
+                gg, piece = pieces.pop(0)
+                ck_quant(gg, piece)
+            if r >= 8:
+                main_mm(r // 8 - 1, 2 * (r % 8))
+                main_mm(r // 8 - 1, 2 * (r % 8) + 1)
+                if r % 8 == 7:
+                    main_evac(r // 8 - 1)
+                    pieces.extend([(0, 2 * (r // 8 - 1)), (0, 2 * (r // 8 - 1) + 1)])
+
+        for tt in range(18):
+            if tt < 16:
+                rope_mm(tt)
+            if tt < 3:
+                w_inter(32 + tt)
+            if tt < 2:
+                w_load(36 + tt)
+            if pieces:
+                gg, piece = pieces.pop(0)
+                ck_inter(gg, piece)
+                ck_quant(gg, piece)
+            if 1 <= tt < 3:
+                w_quant(31 + tt)
+            if tt % 4 == 1 and tt >= 5:
+                rope_math(tt // 4 - 1)
+
+        for i in range(32, 128):
             s, g = divmod(i, 16)
             if i + 6 < 128:
                 w_load(i + 6)
@@ -417,8 +496,8 @@ def tile_multiheadlatentattention_pa_l_kernel(tc, x, cos, sin, wkv_down, w_up, o
                 gg, piece = pieces.pop(0)
                 ck_quant(gg, piece)
             sweep_mm(i)
-            if i % 7 == 3 and i // 7 < 16:
-                rope_store(i // 7)
+            if i % 5 == 4 and (i - 32) // 5 < 16:
+                rope_store((i - 32) // 5)
             if i >= 113:
                 pu(i - 113, i < 127)
             if g == 15:

@@ -15,18 +15,25 @@ SUB = mybir.AluOpType.subtract
 P = 128
 FLOPS = 2 * 2048 * 8192 * 2176 + 2 * 2048 * 2048 * 6144
 
-R4_BUFS = 9
-R2_BUFS = 6
+R4_BUFS = 8
+R2_BUFS = 8
 RING = 6
 UNITS = 64
 X_LEAD = 3
 SORT_LEAD = 2
 QUANT_LAG = 2
 W_LAG = 2
+MAIN_LAG = 3
 
 
 def sorted_unit(u):
-    return u >= 32
+    return u >= 18
+
+
+def unit_tile(u):
+    quarter, a = divmod(u, 4)
+    n, q = divmod(quarter, 4)
+    return 4 * n + a, q
 
 
 def tile_multiheadlatentattention_pa_l_kernel(tc, x, cos, sin, wkv_down, w_up, out_0, out_1):
@@ -61,6 +68,13 @@ def tile_multiheadlatentattention_pa_l_kernel(tc, x, cos, sin, wkv_down, w_up, o
 
         xf = x.flatten_outer_dims()
 
+        def x_loads(r):
+            if r < 7:
+                return [2 * r + 4, 2 * r + 5]
+            if r == 7:
+                return [18, 19, 20, 21]
+            return [u for u in (2 * r + 6, 2 * r + 7) if u < UNITS]
+
         ident = sb.tile([P, P], F32, name="ident", tag="ident", bufs=1, align_bytes=64)
         make_identity(nc, ident[:])
         cos_sb = sb.tile([P, 4, 64], BF16, name="cos_sb", tag="cos_sb", bufs=1, align_bytes=64)
@@ -79,7 +93,7 @@ def tile_multiheadlatentattention_pa_l_kernel(tc, x, cos, sin, wkv_down, w_up, o
         xr, xsd, xt, gw = {}, {}, {}, {}
 
         def load_x(u):
-            tt, q = divmod(u, 4)
+            tt, q = unit_tile(u)
             t = r4([P, 2048], BF16, "xr")
             nc.sync.dma_start(out=t[:], in_=xf[128 * tt : 128 * tt + 128, 2048 * q : 2048 * q + 2048])
             xr[u] = t
@@ -116,7 +130,7 @@ def tile_multiheadlatentattention_pa_l_kernel(tc, x, cos, sin, wkv_down, w_up, o
                 gw[(u, half)] = t
 
         def quant_x(u):
-            tt, q = divmod(u, 4)
+            tt, q = unit_tile(u)
             for half in range(2):
                 t = gw.pop((u, half))
                 for g2 in range(2):
@@ -131,7 +145,7 @@ def tile_multiheadlatentattention_pa_l_kernel(tc, x, cos, sin, wkv_down, w_up, o
         rr, rg = {}, {}
 
         def rope_w_load(g4):
-            t = r4([P, 4, 4, 128], BF16, "rr")
+            t = ck_slot([P, 4, 4, 128], "rr", BF16)
             for gl in range(4):
                 g = 4 * g4 + gl
                 nc.sync.dma_start(
@@ -140,17 +154,17 @@ def tile_multiheadlatentattention_pa_l_kernel(tc, x, cos, sin, wkv_down, w_up, o
             rr[g4] = t
 
         def rope_w_inter(g4):
-            t = r4([P, 4, 128, 4], BF16, "rg")
+            t = ck_slot([P, 4, 128, 4], "rg", BF16)
             nc.vector.tensor_copy(out=t[:], in_=rr.pop(g4)[:].rearrange("p g j c -> p g c j"))
             rg[g4] = t
 
         def rope_w_quant(g4):
             t = rg.pop(g4)
-            if g4 % 2 == 0:
-                wxr[g4 // 2] = r4([P, 8, 128], U32, "wxr")
+            if g4 == 0:
+                wxr[0] = ck_slot([P, 16, 128], "wxr")
             for gl in range(4):
                 nc.vector.quantize_mx(
-                    out=wxr[g4 // 2][:, 4 * (g4 % 2) + gl, :].bitcast(FP8X4),
+                    out=wxr[0][:, 4 * g4 + gl, :].bitcast(FP8X4),
                     scales=wrs[4 * gl : P, g4, :],
                     in_=t[:, gl].rearrange("p c j -> p (c j)"),
                 )
@@ -168,7 +182,7 @@ def tile_multiheadlatentattention_pa_l_kernel(tc, x, cos, sin, wkv_down, w_up, o
                     out=rp[n][:, a, :],
                     lhsT=xc[g][:, cols].bitcast(FP8X4),
                     lhsT_scale=xs[g // 4][k:P, cols],
-                    rhs=wxr[g // 8][:, g % 8, :].bitcast(FP8X4),
+                    rhs=wxr[0][:, g, :].bitcast(FP8X4),
                     rhs_scale=wrs[k:P, g // 4, :],
                     start=(g == 0),
                     stop=(g == 15),
@@ -283,7 +297,7 @@ def tile_multiheadlatentattention_pa_l_kernel(tc, x, cos, sin, wkv_down, w_up, o
             for tl, n in BANK_ORDER[s == 7]:
                 if True:
                     if g == 0:
-                        acc[(tl, n)] = bank((4 + BANK_ORDER[s == 7].index((tl, n))) % 8, [P, 512])
+                        acc[(tl, n)] = bank(((0 if s == 2 else 4) + BANK_ORDER[s == 7].index((tl, n))) % 8, [P, 512])
                     nc.tensor.matmul_mx(
                         out=acc[(tl, n)][:],
                         lhsT=rc[:, 128 * tl : 128 * tl + 128].bitcast(FP8X4),
@@ -413,15 +427,17 @@ def tile_multiheadlatentattention_pa_l_kernel(tc, x, cos, sin, wkv_down, w_up, o
             )
             nc.sync.dma_start(out=out_1[b, rows, 4 * hg : 4 * hg + 4, :].rearrange("l h c -> l (h c)"), in_=vo[:])
 
-        W_ROUND = [(3 * g) // 4 for g in range(16)]
-        ROPE_W_ROUND = {30: 0, 31: 1, 32: 2, 33: 3}
         pieces = []
 
-        for u in range(X_LEAD + 2):
+        for u in range(2):
             load_x(u)
-        sort_x(0)
-        sort_x(1)
-        for r in range(40):
+        for g in range(2):
+            w_load(g)
+        for u in range(2, 4):
+            load_x(u)
+        for g in range(2, 4):
+            w_load(g)
+        for r in range(32 + MAIN_LAG):
             for u in (2 * r - 2, 2 * r - 1):
                 if 0 <= u < UNITS:
                     quant_x(u)
@@ -430,57 +446,41 @@ def tile_multiheadlatentattention_pa_l_kernel(tc, x, cos, sin, wkv_down, w_up, o
                 transpose_x(2 * r + 1)
                 copy_x(2 * r)
                 copy_x(2 * r + 1)
-            for u in (2 * r + X_LEAD + 2, 2 * r + X_LEAD + 3):
-                if u < UNITS:
-                    load_x(u)
-            for g in range(16):
-                if W_ROUND[g] == r:
-                    w_load(g)
-            if r in ROPE_W_ROUND:
-                rope_w_load(ROPE_W_ROUND[r])
-            if r >= 38:
-                w_load(32 + 2 * (r - 38))
-                w_load(33 + 2 * (r - 38))
-            for g in range(16):
-                if W_ROUND[g] + W_LAG == r:
+            for u in x_loads(r):
+                load_x(u)
+            if r < 8:
+                for g in (2 * r, 2 * r + 1):
                     main_w_inter(g, 0)
                     main_w_inter(g, 1)
                     main_w_quant(g, 0)
                     main_w_quant(g, 1)
-            if r - 2 in ROPE_W_ROUND:
-                rope_w_inter(ROPE_W_ROUND[r - 2])
+                for g in (2 * r + 4, 2 * r + 5):
+                    if g < 16:
+                        w_load(g)
+            if 0 <= r - (29 + MAIN_LAG) < 3:
+                w_load(32 + 2 * (r - (29 + MAIN_LAG)))
+                w_load(33 + 2 * (r - (29 + MAIN_LAG)))
+            if 0 <= r - (30 + MAIN_LAG) < 2:
+                w_inter(32 + r - (30 + MAIN_LAG))
             if pieces:
                 ck_inter(pieces[0][0], pieces[0][1])
             for u in (2 * r + 2, 2 * r + 3):
                 if u < UNITS:
                     sort_x(u)
-            if r - 3 in ROPE_W_ROUND:
-                rope_w_quant(ROPE_W_ROUND[r - 3])
+            if r == 31 + MAIN_LAG:
+                w_quant(32)
             if pieces:
                 gg, piece = pieces.pop(0)
                 ck_quant(gg, piece)
-            if r >= 8:
-                main_mm(r // 8 - 1, 2 * (r % 8))
-                main_mm(r // 8 - 1, 2 * (r % 8) + 1)
-                if r % 8 == 7:
-                    main_evac(r // 8 - 1)
-                    pieces.extend([(0, 2 * (r // 8 - 1)), (0, 2 * (r // 8 - 1) + 1)])
-
-        for tt in range(18):
-            if tt < 16:
-                rope_mm(tt)
-            if tt < 3:
-                w_inter(32 + tt)
-            if tt < 2:
-                w_load(36 + tt)
-            if pieces:
-                gg, piece = pieces.pop(0)
-                ck_inter(gg, piece)
-                ck_quant(gg, piece)
-            if 1 <= tt < 3:
-                w_quant(31 + tt)
-            if tt % 4 == 1 and tt >= 5:
-                rope_math(tt // 4 - 1)
+            if r >= MAIN_LAG:
+                n, half_g = divmod(r - MAIN_LAG, 8)
+                main_mm(n, 2 * half_g)
+                main_mm(n, 2 * half_g + 1)
+                if half_g == 7:
+                    main_evac(n)
+                    pieces.extend([(0, 2 * n), (0, 2 * n + 1)])
+        w_inter(34)
+        w_quant(33)
 
         for i in range(32, 128):
             s, g = divmod(i, 16)
@@ -495,15 +495,27 @@ def tile_multiheadlatentattention_pa_l_kernel(tc, x, cos, sin, wkv_down, w_up, o
             if pieces:
                 gg, piece = pieces.pop(0)
                 ck_quant(gg, piece)
+            if s == 2 and g % 3 == 0 and g // 3 < 4:
+                rope_w_load(g // 3)
+            if s == 2 and g % 3 == 2 and g // 3 < 4:
+                rope_w_inter(g // 3)
+            if s == 2 and g % 3 == 0 and 1 <= g // 3 < 5:
+                rope_w_quant(g // 3 - 1)
             sweep_mm(i)
-            if i % 5 == 4 and (i - 32) // 5 < 16:
-                rope_store((i - 32) // 5)
+            if i >= 50 and i % 4 == 2 and (i - 50) // 4 < 16:
+                rope_store((i - 50) // 4)
             if i >= 113:
                 pu(i - 113, i < 127)
             if g == 15:
                 evac(s)
                 if s % 2 == 1:
                     pieces.extend([(s // 2, piece) for piece in range(8)])
+            if i == 47:
+                for tt in range(18):
+                    if tt < 16:
+                        rope_mm(tt)
+                    if tt % 4 == 1 and tt >= 5:
+                        rope_math(tt // 4 - 1)
 
         for gg, piece in pieces:
             ck_inter(gg, piece)

@@ -294,7 +294,7 @@ def tile_multiheadlatentattention_pa_l_kernel(tc, x, cos, sin, wkv_down, w_up, o
             s, g = divmod(i, 16)
             rc, rs = ring.pop(i)
             k = 4 * (g % 4)
-            for tl, n in BANK_ORDER[s == 7]:
+            for tl, n in BANK_ORDER[s == 7 and g == 15]:
                 if True:
                     if g == 0:
                         acc[(tl, n)] = bank(((0 if s == 2 else 4) + BANK_ORDER[s == 7].index((tl, n))) % 8, [P, 512])
@@ -320,6 +320,12 @@ def tile_multiheadlatentattention_pa_l_kernel(tc, x, cos, sin, wkv_down, w_up, o
                     nc.vector.tensor_copy(out=dst, in_=acc.pop((tl, n))[:])
 
         cg = {}
+        last_plane = []
+
+        def ck_plane(gg, cols):
+            if gg == 3:
+                return last_plane[0][:, cols]
+            return cks[4 * gg : P, cols]
 
         def ck_inter(gg, piece):
             n, i2 = divmod(piece, 2)
@@ -330,10 +336,12 @@ def tile_multiheadlatentattention_pa_l_kernel(tc, x, cos, sin, wkv_down, w_up, o
         def ck_quant(gg, piece):
             if piece == 0:
                 ck[gg] = ck_slot([P, 2048], "ck%d" % gg)
+                if gg == 3:
+                    last_plane.append(sb.tile([P, 2048], U8, name="cks3", tag="wxs", bufs=1, align_bytes=64))
             cols = slice(256 * piece, 256 * piece + 256)
             nc.vector.quantize_mx(
                 out=ck[gg][:, cols].bitcast(FP8X4),
-                scales=cks[4 * gg : P, cols],
+                scales=ck_plane(gg, cols),
                 in_=cg.pop(piece)[:].rearrange("p c t -> p (c t)"),
             )
 
@@ -376,26 +384,27 @@ def tile_multiheadlatentattention_pa_l_kernel(tc, x, cos, sin, wkv_down, w_up, o
                 in_=ug.pop(j)[:].rearrange("p s c j -> p (s c j)"),
             )
 
-        def pu(t, inter=True):
-            if inter and 0 <= t - 2 < 48:
+        def pu(t):
+            if 0 <= t - 2 < 48:
                 u_inter(t - 2)
             if 0 <= t - 3 < 48:
                 u_quant(t - 3)
             if t < 48:
                 u_load(t)
 
-        cell = {}
+        cell, outs = {}, {}
+        opened = []
 
-        def up_mm(ci, gg):
-            c, cbl = divmod(ci, 3)
+        def up_mm(c, cbl, gg):
             hg, tt = divmod(c, 16)
             if gg == 0:
-                cell[ci] = bank((ci + 4) % 8, [P, 512])
+                cell[(c, cbl)] = bank((len(opened) + 4) % 8, [P, 512])
+                opened.append((c, cbl))
             cols = slice(128 * tt, 128 * tt + 128)
             nc.tensor.matmul_mx(
-                out=cell[ci][:],
+                out=cell[(c, cbl)][:],
                 lhsT=ck[gg][:, cols].bitcast(FP8X4),
-                lhsT_scale=cks[4 * gg : P, cols],
+                lhsT_scale=ck_plane(gg, cols),
                 rhs=wu[3 * hg + cbl][:, gg, :].bitcast(FP8X4),
                 rhs_scale=wus[hg][4 * gg : P, 512 * cbl : 512 * cbl + 512],
                 start=(gg == 0),
@@ -404,23 +413,27 @@ def tile_multiheadlatentattention_pa_l_kernel(tc, x, cos, sin, wkv_down, w_up, o
 
         K_COLS = (256, 128, 128)
 
-        def up_out(c):
+        def up_empty(c, cbl):
+            if cbl == 0:
+                ko = r2([P, 512], F32, "ko")
+                vo = r4([P, 1024], F32, "vo")
+                outs[c] = (ko, vo)
+            ko, vo = outs[c]
+            src = cell.pop((c, cbl))
+            kc = K_COLS[cbl]
+            k0 = sum(K_COLS[:cbl])
+            v0 = 512 * cbl - k0
+            if cbl == 1 and c >= 4:
+                nc.vector.tensor_copy(out=ko[:, k0 : k0 + kc], in_=src[:, 0:kc])
+                nc.vector.tensor_copy(out=vo[:, v0 : v0 + 512 - kc], in_=src[:, kc:512])
+            else:
+                nc.scalar.copy(out=ko[:, k0 : k0 + kc], in_=src[:, 0:kc])
+                nc.scalar.copy(out=vo[:, v0 : v0 + 512 - kc], in_=src[:, kc:512])
+
+        def up_store(c):
             hg, tt = divmod(c, 16)
             b, a = divmod(tt, 4)
-            ko = r2([P, 512], F32, "ko")
-            vo = r4([P, 1024], F32, "vo")
-            k0, v0 = 0, 0
-            for cbl in range(3):
-                src = cell.pop(3 * c + cbl)
-                kc = K_COLS[cbl]
-                if cbl == 1:
-                    nc.vector.tensor_copy(out=ko[:, k0 : k0 + kc], in_=src[:, 0:kc])
-                    nc.vector.tensor_copy(out=vo[:, v0 : v0 + 512 - kc], in_=src[:, kc:512])
-                else:
-                    nc.scalar.copy(out=ko[:, k0 : k0 + kc], in_=src[:, 0:kc])
-                    nc.scalar.copy(out=vo[:, v0 : v0 + 512 - kc], in_=src[:, kc:512])
-                k0 += kc
-                v0 += 512 - kc
+            ko, vo = outs.pop(c)
             rows = slice(128 * a, 128 * a + 128)
             nc.sync.dma_start(
                 out=out_0[b, rows, 4 * hg : 4 * hg + 4, 0:128], in_=ko[:].rearrange("p (h c) -> p h c", h=4)
@@ -504,8 +517,8 @@ def tile_multiheadlatentattention_pa_l_kernel(tc, x, cos, sin, wkv_down, w_up, o
             sweep_mm(i)
             if i >= 50 and i % 4 == 2 and (i - 50) // 4 < 16:
                 rope_store((i - 50) // 4)
-            if i >= 113:
-                pu(i - 113, i < 127)
+            if 113 <= i <= 124:
+                pu(i - 113)
             if g == 15:
                 evac(s)
                 if s % 2 == 1:
@@ -517,30 +530,36 @@ def tile_multiheadlatentattention_pa_l_kernel(tc, x, cos, sin, wkv_down, w_up, o
                     if tt % 4 == 1 and tt >= 5:
                         rope_math(tt // 4 - 1)
 
-        for gg, piece in pieces:
-            ck_inter(gg, piece)
-            if piece > 0:
-                ck_quant(gg, piece - 1)
-            if piece == 2:
-                u_inter(12)
-        ck_quant(3, 7)
+        ck_inter(3, 0)
+        ck_inter(3, 1)
+        ck_quant(3, 0)
+        ck_quant(3, 1)
+        for t in range(12, 15):
+            pu(t)
+            ck_inter(3, 2 * (t - 11))
+            ck_inter(3, 2 * (t - 11) + 1)
+            ck_quant(3, 2 * (t - 11))
+            ck_quant(3, 2 * (t - 11) + 1)
 
-        for gg in range(3):
-            for ci in range(8):
-                up_mm(ci, gg)
-        for ci in range(8):
-            up_mm(ci, 3)
-        up_out(0)
-        up_out(1)
-        pu(15)
-        pu(16)
+        first = [(c, cbl) for c in range(4) for cbl in range(2)]
         for gg in range(4):
-            up_mm(8, gg)
-        up_out(2)
-        pu(17)
-        for c in range(3, 64):
+            for c, cbl in first:
+                up_mm(c, cbl, gg)
+        for c, cbl in first:
+            up_empty(c, cbl)
+        todo = list(range(15, 51))
+        for c in range(4):
+            for gg in range(4):
+                up_mm(c, 2, gg)
+            up_empty(c, 2)
+            up_store(c)
+            pu(todo.pop(0))
+        for c in range(4, 64):
+            for gg in range(4):
+                for cbl in range(3):
+                    up_mm(c, cbl, gg)
             for cbl in range(3):
-                for gg in range(4):
-                    up_mm(3 * c + cbl, gg)
-            up_out(c)
-            pu(15 + c)
+                up_empty(c, cbl)
+            up_store(c)
+            if todo and c % 5 != 4:
+                pu(todo.pop(0))

from contextlib import ExitStack

import concourse.mybir as mybir
from concourse.masks import make_identity

F32 = mybir.dt.float32
BF16 = mybir.dt.bfloat16
U32 = mybir.dt.uint32
U8 = mybir.dt.uint8
FP8X4 = mybir.dt.float8_e4m3fn_x4
MULT = mybir.AluOpType.mult
ADD = mybir.AluOpType.add
SUB = mybir.AluOpType.subtract

P = 128
FLOPS = 2 * 2048 * 8192 * 2176 + 2 * 2048 * 2048 * 6144

R4_BUFS = 8
R2_BUFS = 8
RING = 6
UNITS = 64
X_LEAD = 3
SORT_LEAD = 2
QUANT_LAG = 2
W_LAG = 2
MAIN_LAG = 3


def sorted_unit(u):
    return u >= 18


def unit_tile(u):
    quarter, a = divmod(u, 4)
    n, q = divmod(quarter, 4)
    return 4 * n + a, q


def tile_multiheadlatentattention_pa_l_kernel(tc, x, cos, sin, wkv_down, w_up, out_0, out_1):
    nc = tc.nc
    with ExitStack() as ctx:
        sb = ctx.enter_context(tc.tile_pool(name="sb", bufs=1))
        ps = ctx.enter_context(tc.psum_pool(name="ps", bufs=1))

        def r4(shape, dtype, name):
            t = sb.tile(shape, dtype, name=name, tag="r4", bufs=R4_BUFS, align_bytes=64)
            return t

        def r2(shape, dtype, name):
            t = sb.tile(shape, dtype, name=name, tag="r2", bufs=R2_BUFS, align_bytes=64)
            return t

        def big(shape, dtype, name):
            t = sb.tile(shape, dtype, name=name, tag="xc", bufs=16, align_bytes=64)
            return t

        def plane(shape, name):
            t = sb.tile(shape, U8, name=name, tag="xs", bufs=4, align_bytes=64)
            return t

        def ck_slot(shape, name, dtype=U32):
            t = sb.tile(shape, dtype, name=name, tag="ck", bufs=5, align_bytes=64)
            return t

        def bank(i, shape):
            t = ps.tile(shape, F32, name="bank%d" % i, tag="b%d" % i, bufs=1)
            return t

        xf = x.flatten_outer_dims()

        def x_loads(r):
            if r < 7:
                return [2 * r + 4, 2 * r + 5]
            if r == 7:
                return [18, 19, 20, 21]
            return [u for u in (2 * r + 6, 2 * r + 7) if u < UNITS]

        ident = sb.tile([P, P], F32, name="ident", tag="ident", bufs=1, align_bytes=64)
        make_identity(nc, ident[:])
        cos_sb = sb.tile([P, 4, 64], BF16, name="cos_sb", tag="cos_sb", bufs=1, align_bytes=64)
        sin_sb = sb.tile([P, 4, 64], BF16, name="sin_sb", tag="sin_sb", bufs=1, align_bytes=64)
        nc.scalar.dma_start(out=cos_sb[:], in_=cos.rearrange("(a p) j -> p a j", p=P))
        nc.scalar.dma_start(out=sin_sb[:], in_=sin.rearrange("(a p) j -> p a j", p=P))
        ctx.enter_context(tc.manual_schedule())

        xc = [big([P, 2048], U32, "xc%d" % g) for g in range(16)]
        xs = [plane([P, 2048], "xs%d" % gq) for gq in range(4)]
        cks = sb.tile([P, 2048], U8, name="cks", tag="cks", bufs=1, align_bytes=64)
        wxr = {}
        wxs = sb.tile([P, 4, 512], U8, name="wxs", tag="wxs", bufs=1, align_bytes=64)
        wrs = sb.tile([P, 4, 128], U8, name="wrs", tag="wrs", bufs=1, align_bytes=64)

        xr, xsd, xt, gw = {}, {}, {}, {}

        def load_x(u):
            tt, q = unit_tile(u)
            t = r4([P, 2048], BF16, "xr")
            nc.sync.dma_start(out=t[:], in_=xf[128 * tt : 128 * tt + 128, 2048 * q : 2048 * q + 2048])
            xr[u] = t

        def sort_x(u):
            if sorted_unit(u):
                t = r4([P, 4, 2, 128], F32, "xsd")
                nc.vector.tensor_copy(
                    out=t[:], in_=xr.pop(u)[:].bitcast(F32).rearrange("a (g p u) -> a g u p", g=4, u=2)
                )
                xsd[u] = t

        def transpose_x(u):
            if sorted_unit(u):
                src = xsd.pop(u)
            else:
                src = xr.pop(u)[:].bitcast(F32)
            for half in range(2):
                b = bank((2 * u + half) % 4, [P, 2, 2, 128])
                for g2 in range(2):
                    gl = 2 * half + g2
                    for uu in range(2):
                        if sorted_unit(u):
                            words = src[:, gl, uu, :]
                        else:
                            words = src[:, 256 * gl + uu : 256 * (gl + 1) : 2]
                        nc.tensor.transpose(b[:, g2, uu, :], words, ident[:])
                xt[(u, half)] = b

        def copy_x(u):
            for half in range(2):
                t = r2([P, 2, 128, 2], F32, "gw")
                nc.scalar.copy(out=t[:], in_=xt.pop((u, half))[:].rearrange("p g u c -> p g c u"))
                gw[(u, half)] = t

        def quant_x(u):
            tt, q = unit_tile(u)
            for half in range(2):
                t = gw.pop((u, half))
                for g2 in range(2):
                    g = 4 * q + 2 * half + g2
                    k = 4 * (g % 4)
                    nc.vector.quantize_mx(
                        out=xc[g][:, 128 * tt : 128 * tt + 128].bitcast(FP8X4),
                        scales=xs[g // 4][k:P, 128 * tt : 128 * tt + 128],
                        in_=t[:, g2].rearrange("p c u -> p (c u)").bitcast(BF16),
                    )

        rr, rg = {}, {}

        def rope_w_load(g4):
            t = ck_slot([P, 4, 4, 128], "rr", BF16)
            for gl in range(4):
                g = 4 * g4 + gl
                nc.sync.dma_start(
                    out=t[:, gl], in_=wkv_down[512 * g : 512 * g + 512, 2048:2176].rearrange("(p j) c -> p j c", j=4)
                )
            rr[g4] = t

        def rope_w_inter(g4):
            t = ck_slot([P, 4, 128, 4], "rg", BF16)
            nc.vector.tensor_copy(out=t[:], in_=rr.pop(g4)[:].rearrange("p g j c -> p g c j"))
            rg[g4] = t

        def rope_w_quant(g4):
            t = rg.pop(g4)
            if g4 == 0:
                wxr[0] = ck_slot([P, 16, 128], "wxr")
            for gl in range(4):
                nc.vector.quantize_mx(
                    out=wxr[0][:, 4 * g4 + gl, :].bitcast(FP8X4),
                    scales=wrs[4 * gl : P, g4, :],
                    in_=t[:, gl].rearrange("p c j -> p (c j)"),
                )

        rp, krs = {}, {}

        def rope_mm(tt):
            n, a = divmod(tt, 4)
            if a == 0:
                rp[n] = bank(n, [P, 4, 128])
            cols = slice(128 * tt, 128 * tt + 128)
            for g in range(16):
                k = 4 * (g % 4)
                nc.tensor.matmul_mx(
                    out=rp[n][:, a, :],
                    lhsT=xc[g][:, cols].bitcast(FP8X4),
                    lhsT_scale=xs[g // 4][k:P, cols],
                    rhs=wxr[0][:, g, :].bitcast(FP8X4),
                    rhs_scale=wrs[k:P, g // 4, :],
                    start=(g == 0),
                    stop=(g == 15),
                )

        def rope_math(n):
            r = rp.pop(n)[:].rearrange("p a (j e) -> p a j e", e=2)
            if n == 0:
                krs[0] = ck_slot([P, 16, 64, 2], "krall", F32)
            kr = krs[0][:, 4 * n : 4 * n + 4]
            tmp = [sb.tile([P, 4, 64], F32, name="tmp%d" % i, tag="rc", bufs=RING, align_bytes=64) for i in range(4)]
            nc.vector.tensor_tensor(out=tmp[0][:], in0=r[:, :, :, 0], in1=cos_sb[:], op=MULT)
            nc.vector.tensor_tensor(out=tmp[1][:], in0=r[:, :, :, 1], in1=sin_sb[:], op=MULT)
            nc.vector.tensor_tensor(out=tmp[2][:], in0=r[:, :, :, 0], in1=sin_sb[:], op=MULT)
            nc.vector.tensor_tensor(out=tmp[3][:], in0=r[:, :, :, 1], in1=cos_sb[:], op=MULT)
            nc.vector.tensor_tensor(out=kr[:, :, :, 0], in0=tmp[0][:], in1=tmp[1][:], op=SUB)
            nc.vector.tensor_tensor(out=kr[:, :, :, 1], in0=tmp[2][:], in1=tmp[3][:], op=ADD)

        def rope_store(tt):
            n, a = divmod(tt, 4)
            nc.sync.dma_start(
                out=out_0[n, 128 * a : 128 * a + 128, :, 128:256],
                in_=krs[0][:, tt].rearrange("p j e -> p (j e)").unsqueeze(1).to_broadcast([P, 16, 128]),
            )

        wr, wg, ring = {}, {}, {}
        st, ck = {}, {}

        def w_load(i):
            s, g = divmod(i, 16)
            t = r4([P, 4, 512], BF16, "wr")
            gg = s // 2
            nc.sync.dma_start(
                out=t[:],
                in_=wkv_down[512 * g : 512 * g + 512, 512 * gg : 512 * gg + 512].rearrange("(p j) c -> p j c", j=4),
            )
            wr[i] = t

        def w_inter(i):
            h = (i // 16) % 2
            t = r2([P, 1024], BF16, "wg")
            dst = t[:].rearrange("p (t m j) -> p t m j", t=2, j=4)
            src = wr.pop(i)[:].rearrange("p j (m t) -> p t m j", t=4)[:, 2 * h : 2 * h + 2]
            if i % 2 == 0 or i >= 112:
                nc.scalar.copy(out=dst, in_=src)
            else:
                nc.vector.tensor_copy(out=dst, in_=src)
            wg[i] = t

        def w_quant(i):
            rc = sb.tile([P, 256], U32, name="rc", tag="rc", bufs=RING, align_bytes=64)
            rs = sb.tile([P, 256], U8, name="rs", tag="rs", bufs=RING, align_bytes=64)
            nc.vector.quantize_mx(out=rc[:].bitcast(FP8X4), scales=rs[:], in_=wg.pop(i)[:])
            ring[i] = (rc, rs)

        wxh = {}

        def main_w_inter(g, h):
            t = r2([P, 1024], BF16, "wg")
            dst = t[:].rearrange("p (t m j) -> p t m j", t=2, j=4)
            src = wr[g][:].rearrange("p j (m t) -> p t m j", t=4)[:, 2 * h : 2 * h + 2]
            if h == 0:
                nc.scalar.copy(out=dst, in_=src)
            else:
                nc.vector.tensor_copy(out=dst, in_=src)
                wr.pop(g)
            wg[(g, h)] = t

        def main_w_quant(g, h):
            if g % 8 == 0:
                wxh[(h, g // 8)] = ck_slot([P, 8, 256], "wxh")
            nc.vector.quantize_mx(
                out=wxh[(h, g // 8)][:, g % 8, :].bitcast(FP8X4),
                scales=wxs[4 * (g % 4) : P, g // 4, 256 * h : 256 * h + 256],
                in_=wg.pop((g, h))[:],
            )

        def main_mm(n, g):
            k = 4 * (g % 4)
            for t in range(4):
                h, tl = divmod(t, 2)
                if g == 0:
                    acc[(t, n)] = bank(4 + t, [P, 512])
                nc.tensor.matmul_mx(
                    out=acc[(t, n)][:],
                    lhsT=wxh[(h, g // 8)][:, g % 8, 128 * tl : 128 * tl + 128].bitcast(FP8X4),
                    lhsT_scale=wxs[k:P, g // 4, 256 * h + 128 * tl : 256 * h + 128 * tl + 128],
                    rhs=xc[g][:, 512 * n : 512 * n + 512].bitcast(FP8X4),
                    rhs_scale=xs[g // 4][k:P, 512 * n : 512 * n + 512],
                    start=(g == 0),
                    stop=(g == 15),
                )

        def main_evac(n):
            st[n] = r4([P, 4, 512], BF16, "st")
            for t in range(4):
                if t % 2 == 0:
                    nc.scalar.copy(out=st[n][:, t, :], in_=acc.pop((t, n))[:])
                else:
                    nc.vector.tensor_copy(out=st[n][:, t, :], in_=acc.pop((t, n))[:])

        acc = {}
        BANK_ORDER = {
            False: [(tl, n) for tl in range(2) for n in range(4)],
            True: [(tl, n) for n in range(4) for tl in range(2)],
        }

        def sweep_mm(i):
            s, g = divmod(i, 16)
            rc, rs = ring.pop(i)
            k = 4 * (g % 4)
            for tl, n in BANK_ORDER[s == 7 and g == 15]:
                if True:
                    if g == 0:
                        acc[(tl, n)] = bank(((0 if s == 2 else 4) + BANK_ORDER[s == 7].index((tl, n))) % 8, [P, 512])
                    nc.tensor.matmul_mx(
                        out=acc[(tl, n)][:],
                        lhsT=rc[:, 128 * tl : 128 * tl + 128].bitcast(FP8X4),
                        lhsT_scale=rs[:, 128 * tl : 128 * tl + 128],
                        rhs=xc[g][:, 512 * n : 512 * n + 512].bitcast(FP8X4),
                        rhs_scale=xs[g // 4][k:P, 512 * n : 512 * n + 512],
                        start=(g == 0),
                        stop=(g == 15),
                    )

        def evac(s):
            h = s % 2
            for tl, n in BANK_ORDER[s == 7]:
                if h == 0 and tl == 0:
                    st[n] = r4([P, 4, 512], BF16, "st")
                dst = st[n][:, 2 * h + tl, :]
                if n % 2 == 0 or s == 7:
                    nc.scalar.copy(out=dst, in_=acc.pop((tl, n))[:])
                else:
                    nc.vector.tensor_copy(out=dst, in_=acc.pop((tl, n))[:])

        cg = {}
        last_plane = []

        def ck_plane(gg, cols):
            if gg == 3:
                return last_plane[0][:, cols]
            return cks[4 * gg : P, cols]

        def ck_inter(gg, piece):
            n, i2 = divmod(piece, 2)
            t = r2([P, 256, 4], BF16, "cg")
            nc.vector.tensor_copy(out=t[:], in_=st[n][:, :, 256 * i2 : 256 * i2 + 256].rearrange("p t c -> p c t"))
            cg[piece] = t

        def ck_quant(gg, piece):
            if piece == 0:
                ck[gg] = ck_slot([P, 2048], "ck%d" % gg)
                if gg == 3:
                    last_plane.append(sb.tile([P, 2048], U8, name="cks3", tag="wxs", bufs=1, align_bytes=64))
            cols = slice(256 * piece, 256 * piece + 256)
            nc.vector.quantize_mx(
                out=ck[gg][:, cols].bitcast(FP8X4),
                scales=ck_plane(gg, cols),
                in_=cg.pop(piece)[:].rearrange("p c t -> p (c t)"),
            )

        UNIT_MOVES = (
            ((0, 2, 0, 3), (2, 2, 1, 1)),
            ((0, 1, 2, 1), (1, 2, 0, 1), (3, 1, 3, 1)),
            ((0, 1, 1, 1), (1, 1, 0, 1), (2, 2, 2, 1)),
        )
        ur, ug, wu, wus = {}, {}, {}, {}

        def u_load(j):
            cb, gg = divmod(j, 4)
            t = big([P, 4, 512], BF16, "ur")
            nc.sync.dma_start(
                out=t[:],
                in_=w_up[512 * gg : 512 * gg + 512, 512 * cb : 512 * cb + 512].rearrange("(p j) c -> p j c", j=4),
            )
            ur[j] = t

        def u_inter(j):
            cb = j // 4
            src = ur.pop(j)[:].rearrange("p j (s c) -> p s c j", s=4)
            t = big([P, 4, 128, 4], BF16, "ug")
            for d0, cnt, s0, step in UNIT_MOVES[cb % 3]:
                if j < 12 and j % 3 == 2:
                    nc.scalar.copy(out=t[:, d0 : d0 + cnt], in_=src[:, s0 : s0 + (cnt - 1) * step + 1 : step])
                else:
                    nc.vector.tensor_copy(out=t[:, d0 : d0 + cnt], in_=src[:, s0 : s0 + (cnt - 1) * step + 1 : step])
            ug[j] = t

        def u_quant(j):
            cb, gg = divmod(j, 4)
            if gg == 0:
                wu[cb] = big([P, 4, 512], U32, "wu%d" % cb)
                if cb % 3 == 0:
                    wus[cb // 3] = plane([P, 1536], "wus%d" % (cb // 3))
            nc.vector.quantize_mx(
                out=wu[cb][:, gg, :].bitcast(FP8X4),
                scales=wus[cb // 3][4 * gg : P, 512 * (cb % 3) : 512 * (cb % 3) + 512],
                in_=ug.pop(j)[:].rearrange("p s c j -> p (s c j)"),
            )

        def pu(t):
            if 0 <= t - 2 < 48:
                u_inter(t - 2)
            if 0 <= t - 3 < 48:
                u_quant(t - 3)
            if t < 48:
                u_load(t)

        cell, outs = {}, {}
        opened = []

        def up_mm(c, cbl, gg):
            hg, tt = divmod(c, 16)
            if gg == 0:
                cell[(c, cbl)] = bank((len(opened) + 4) % 8, [P, 512])
                opened.append((c, cbl))
            cols = slice(128 * tt, 128 * tt + 128)
            nc.tensor.matmul_mx(
                out=cell[(c, cbl)][:],
                lhsT=ck[gg][:, cols].bitcast(FP8X4),
                lhsT_scale=ck_plane(gg, cols),
                rhs=wu[3 * hg + cbl][:, gg, :].bitcast(FP8X4),
                rhs_scale=wus[hg][4 * gg : P, 512 * cbl : 512 * cbl + 512],
                start=(gg == 0),
                stop=(gg == 3),
            )

        K_COLS = (256, 128, 128)

        def up_empty(c, cbl):
            if cbl == 0:
                ko = r2([P, 512], F32, "ko")
                vo = r4([P, 1024], F32, "vo")
                outs[c] = (ko, vo)
            ko, vo = outs[c]
            src = cell.pop((c, cbl))
            kc = K_COLS[cbl]
            k0 = sum(K_COLS[:cbl])
            v0 = 512 * cbl - k0
            if cbl == 1 and c >= 4:
                nc.vector.tensor_copy(out=ko[:, k0 : k0 + kc], in_=src[:, 0:kc])
                nc.vector.tensor_copy(out=vo[:, v0 : v0 + 512 - kc], in_=src[:, kc:512])
            else:
                nc.scalar.copy(out=ko[:, k0 : k0 + kc], in_=src[:, 0:kc])
                nc.scalar.copy(out=vo[:, v0 : v0 + 512 - kc], in_=src[:, kc:512])

        def up_store(c):
            hg, tt = divmod(c, 16)
            b, a = divmod(tt, 4)
            ko, vo = outs.pop(c)
            rows = slice(128 * a, 128 * a + 128)
            nc.sync.dma_start(
                out=out_0[b, rows, 4 * hg : 4 * hg + 4, 0:128], in_=ko[:].rearrange("p (h c) -> p h c", h=4)
            )
            nc.sync.dma_start(out=out_1[b, rows, 4 * hg : 4 * hg + 4, :].rearrange("l h c -> l (h c)"), in_=vo[:])

        pieces = []

        for u in range(2):
            load_x(u)
        for g in range(2):
            w_load(g)
        for u in range(2, 4):
            load_x(u)
        for g in range(2, 4):
            w_load(g)
        for r in range(32 + MAIN_LAG):
            for u in (2 * r - 2, 2 * r - 1):
                if 0 <= u < UNITS:
                    quant_x(u)
            if r < 32:
                transpose_x(2 * r)
                transpose_x(2 * r + 1)
                copy_x(2 * r)
                copy_x(2 * r + 1)
            for u in x_loads(r):
                load_x(u)
            if r < 8:
                for g in (2 * r, 2 * r + 1):
                    main_w_inter(g, 0)
                    main_w_inter(g, 1)
                    main_w_quant(g, 0)
                    main_w_quant(g, 1)
                for g in (2 * r + 4, 2 * r + 5):
                    if g < 16:
                        w_load(g)
            if 0 <= r - (29 + MAIN_LAG) < 3:
                w_load(32 + 2 * (r - (29 + MAIN_LAG)))
                w_load(33 + 2 * (r - (29 + MAIN_LAG)))
            if 0 <= r - (30 + MAIN_LAG) < 2:
                w_inter(32 + r - (30 + MAIN_LAG))
            if pieces:
                ck_inter(pieces[0][0], pieces[0][1])
            for u in (2 * r + 2, 2 * r + 3):
                if u < UNITS:
                    sort_x(u)
            if r == 31 + MAIN_LAG:
                w_quant(32)
            if pieces:
                gg, piece = pieces.pop(0)
                ck_quant(gg, piece)
            if r >= MAIN_LAG:
                n, half_g = divmod(r - MAIN_LAG, 8)
                main_mm(n, 2 * half_g)
                main_mm(n, 2 * half_g + 1)
                if half_g == 7:
                    main_evac(n)
                    pieces.extend([(0, 2 * n), (0, 2 * n + 1)])
        w_inter(34)
        w_quant(33)

        for i in range(32, 128):
            s, g = divmod(i, 16)
            if i + 6 < 128:
                w_load(i + 6)
            if i + 3 < 128:
                w_inter(i + 3)
            if pieces:
                ck_inter(pieces[0][0], pieces[0][1])
            if i + 2 < 128:
                w_quant(i + 2)
            if pieces:
                gg, piece = pieces.pop(0)
                ck_quant(gg, piece)
            if s == 2 and g % 3 == 0 and g // 3 < 4:
                rope_w_load(g // 3)
            if s == 2 and g % 3 == 2 and g // 3 < 4:
                rope_w_inter(g // 3)
            if s == 2 and g % 3 == 0 and 1 <= g // 3 < 5:
                rope_w_quant(g // 3 - 1)
            sweep_mm(i)
            if i >= 50 and i % 4 == 2 and (i - 50) // 4 < 16:
                rope_store((i - 50) // 4)
            if 113 <= i <= 124:
                pu(i - 113)
            if g == 15:
                evac(s)
                if s % 2 == 1:
                    pieces.extend([(s // 2, piece) for piece in range(8)])
            if i == 47:
                for tt in range(18):
                    if tt < 16:
                        rope_mm(tt)
                    if tt % 4 == 1 and tt >= 5:
                        rope_math(tt // 4 - 1)

        ck_inter(3, 0)
        ck_inter(3, 1)
        ck_quant(3, 0)
        ck_quant(3, 1)
        for t in range(12, 15):
            pu(t)
            ck_inter(3, 2 * (t - 11))
            ck_inter(3, 2 * (t - 11) + 1)
            ck_quant(3, 2 * (t - 11))
            ck_quant(3, 2 * (t - 11) + 1)

        first = [(c, cbl) for c in range(4) for cbl in range(2)]
        for gg in range(4):
            for c, cbl in first:
                up_mm(c, cbl, gg)
        for c, cbl in first:
            up_empty(c, cbl)
        todo = list(range(15, 51))
        for c in range(4):
            for gg in range(4):
                up_mm(c, 2, gg)
            up_empty(c, 2)
            up_store(c)
            pu(todo.pop(0))
        for c in range(4, 64):
            for gg in range(4):
                for cbl in range(3):
                    up_mm(c, cbl, gg)
            for cbl in range(3):
                up_empty(c, cbl)
            up_store(c)
            if todo and c % 5 != 4:
                pu(todo.pop(0))
